import numpy as np
import ml_dtypes

BF16 = ml_dtypes.bfloat16


def bf(x):
    return np.asarray(x, np.float32).astype(BF16)


def f32(x):
    return np.asarray(x, np.float32)


def f64(x):
    return np.asarray(x).astype(np.float64)


def striped(idx):
    return np.tile(idx.reshape(-1, 16).T, (8, 1))


C, S, A, Q, N = 512, 1024, 8, 512, 4096


def setup_inputs():
    idx = np.concatenate([np.random.permutation(S)[:Q] for _ in range(A)])
    return {"x": f32(0.5 * np.random.standard_normal((C, S))), "b": f32(0.2 * np.random.standard_normal((C, 1))), "offs": striped(idx)}


def reference(x, b, offs):
    idx = offs[:16].T.reshape(-1)
    acc = f64(x)[:, idx].reshape(C, A, Q).sum(axis=1) + f64(b)
    return np.maximum(acc, 0.0)

@@ -1,0 +1,41 @@
+import concourse.mybir as mybir
+
+F32 = mybir.dt.float32
+U16 = mybir.dt.uint16
+ADD = mybir.AluOpType.add
+RELU = mybir.ActivationFunctionType.Relu
+
+P = 128
+C, S = 512, 1024
+A, Q = 8, 512
+BLOCKS = C // P
+RUN_COLUMNS = Q // 16
+
+
+def tile_nnueevaluator_kernel(tc, x, b, offs, out):
+    nc = tc.nc
+    x_blocks = x.rearrange("(p k) s -> k p s", k=BLOCKS)
+    out_blocks = out.rearrange("(p k) q -> k p q", k=BLOCKS)
+    with (
+        tc.tile_pool(name="held", bufs=1) as held,
+        tc.tile_pool(name="sums", bufs=4) as sums,
+    ):
+        offsets = held.tile([P, A * RUN_COLUMNS], U16, name="offsets")
+        nc.sync.dma_start(offsets[:], offs)
+        bias = held.tile([P, BLOCKS], F32, name="bias")
+        nc.sync.dma_start(bias[:], b.rearrange("(p k) o -> p (k o)", k=BLOCKS))
+        windows = [held.tile([P, S], F32, name=f"window{k}") for k in range(BLOCKS)]
+        for k in range(BLOCKS):
+            nc.scalar.dma_start(windows[k][:], x_blocks[k])
+
+        for k in range(BLOCKS):
+            acc = sums.tile([P, Q], F32, name="acc")
+            nc.gpsimd.tensor_copy(acc[:], bias[:, k : k + 1].to_broadcast([P, Q]))
+            for a in range(A):
+                picked = windows[k][:].indirect(offsets[:, a * RUN_COLUMNS : (a + 1) * RUN_COLUMNS])
+                grown = sums.tile([P, Q], F32, name="acc")
+                nc.vector.tensor_tensor(grown[:], picked, acc[:], ADD)
+                acc = grown
+            result = sums.tile([P, Q], F32, name="result")
+            nc.scalar.activation(result[:], acc[:], RELU)
+            nc.sync.dma_start(out_blocks[k], result[:])

@@ -18,7 +18,7 @@ def tile_nnueevaluator_kernel(tc, x, b, offs, out):
     out_blocks = out.rearrange("(p k) q -> k p q", k=BLOCKS)
     with (
         tc.tile_pool(name="held", bufs=1) as held,
-        tc.tile_pool(name="sums", bufs=4) as sums,
+        tc.tile_pool(name="sums", bufs=8) as sums,
     ):
         offsets = held.tile([P, A * RUN_COLUMNS], U16, name="offsets")
         nc.sync.dma_start(offsets[:], offs)
@@ -28,14 +28,18 @@ def tile_nnueevaluator_kernel(tc, x, b, offs, out):
         for k in range(BLOCKS):
             nc.scalar.dma_start(windows[k][:], x_blocks[k])
 
-        for k in range(BLOCKS):
-            acc = sums.tile([P, Q], F32, name="acc")
-            nc.gpsimd.tensor_copy(acc[:], bias[:, k : k + 1].to_broadcast([P, Q]))
+        for pair in range(0, BLOCKS, 2):
+            acc = {}
+            for k in (pair, pair + 1):
+                acc[k] = sums.tile([P, Q], F32, name="acc")
+                nc.gpsimd.tensor_copy(acc[k][:], bias[:, k : k + 1].to_broadcast([P, Q]))
             for a in range(A):
-                picked = windows[k][:].indirect(offsets[:, a * RUN_COLUMNS : (a + 1) * RUN_COLUMNS])
-                grown = sums.tile([P, Q], F32, name="acc")
-                nc.vector.tensor_tensor(grown[:], picked, acc[:], ADD)
-                acc = grown
-            result = sums.tile([P, Q], F32, name="result")
-            nc.scalar.activation(result[:], acc[:], RELU)
-            nc.sync.dma_start(out_blocks[k], result[:])
+                for k in (pair, pair + 1):
+                    picked = windows[k][:].indirect(offsets[:, a * RUN_COLUMNS : (a + 1) * RUN_COLUMNS])
+                    grown = sums.tile([P, Q], F32, name="acc")
+                    nc.vector.tensor_tensor(grown[:], picked, acc[k][:], ADD)
+                    acc[k] = grown
+            for k in (pair, pair + 1):
+                result = sums.tile([P, Q], F32, name="result")
+                nc.scalar.activation(result[:], acc[k][:], RELU)
+                nc.sync.dma_start(out_blocks[k], result[:])

@@ -3,6 +3,7 @@ import concourse.mybir as mybir
 F32 = mybir.dt.float32
 U16 = mybir.dt.uint16
 ADD = mybir.AluOpType.add
+COPY = mybir.ActivationFunctionType.Copy
 RELU = mybir.ActivationFunctionType.Relu
 
 P = 128
@@ -18,7 +19,7 @@ def tile_nnueevaluator_kernel(tc, x, b, offs, out):
     out_blocks = out.rearrange("(p k) q -> k p q", k=BLOCKS)
     with (
         tc.tile_pool(name="held", bufs=1) as held,
-        tc.tile_pool(name="sums", bufs=8) as sums,
+        tc.tile_pool(name="sums", bufs=6) as sums,
     ):
         offsets = held.tile([P, A * RUN_COLUMNS], U16, name="offsets")
         nc.sync.dma_start(offsets[:], offs)
@@ -28,15 +29,15 @@ def tile_nnueevaluator_kernel(tc, x, b, offs, out):
         for k in range(BLOCKS):
             nc.scalar.dma_start(windows[k][:], x_blocks[k])
 
+        acc = [held.tile([P, Q], F32, name=f"start{k}") for k in range(BLOCKS)]
+        for k in range(BLOCKS):
+            nc.scalar.activation(acc[k][:], bias[:, k : k + 1].to_broadcast([P, Q]), COPY)
+
         for pair in range(0, BLOCKS, 2):
-            acc = {}
-            for k in (pair, pair + 1):
-                acc[k] = sums.tile([P, Q], F32, name="acc")
-                nc.gpsimd.tensor_copy(acc[k][:], bias[:, k : k + 1].to_broadcast([P, Q]))
             for a in range(A):
                 for k in (pair, pair + 1):
                     picked = windows[k][:].indirect(offsets[:, a * RUN_COLUMNS : (a + 1) * RUN_COLUMNS])
-                    grown = sums.tile([P, Q], F32, name="acc")
+                    grown = sums.tile([P, Q], F32, name="grown")
                     nc.vector.tensor_tensor(grown[:], picked, acc[k][:], ADD)
                     acc[k] = grown
             for k in (pair, pair + 1):

@@ -21,10 +21,10 @@ def tile_nnueevaluator_kernel(tc, x, b, offs, out):
         tc.tile_pool(name="held", bufs=1) as held,
         tc.tile_pool(name="sums", bufs=6) as sums,
     ):
-        offsets = held.tile([P, A * RUN_COLUMNS], U16, name="offsets")
-        nc.sync.dma_start(offsets[:], offs)
         bias = held.tile([P, BLOCKS], F32, name="bias")
         nc.sync.dma_start(bias[:], b.rearrange("(p k) o -> p (k o)", k=BLOCKS))
+        offsets = held.tile([P, A * RUN_COLUMNS], U16, name="offsets")
+        nc.sync.dma_start(offsets[:], offs)
         windows = [held.tile([P, S], F32, name=f"window{k}") for k in range(BLOCKS)]
         for k in range(BLOCKS):
             nc.scalar.dma_start(windows[k][:], x_blocks[k])

@@ -10,7 +10,8 @@ P = 128
 C, S = 512, 1024
 A, Q = 8, 512
 BLOCKS = C // P
-RUN_COLUMNS = Q // 16
+WHOLE_RUN = ((0, Q),)
+HALVES = ((0, Q // 2), (Q // 2, Q))
 
 
 def tile_nnueevaluator_kernel(tc, x, b, offs, out):
@@ -23,7 +24,7 @@ def tile_nnueevaluator_kernel(tc, x, b, offs, out):
     ):
         bias = held.tile([P, BLOCKS], F32, name="bias")
         nc.sync.dma_start(bias[:], b.rearrange("(p k) o -> p (k o)", k=BLOCKS))
-        offsets = held.tile([P, A * RUN_COLUMNS], U16, name="offsets")
+        offsets = held.tile([P, A * Q // 16], U16, name="offsets")
         nc.sync.dma_start(offsets[:], offs)
         windows = [held.tile([P, S], F32, name=f"window{k}") for k in range(BLOCKS)]
         for k in range(BLOCKS):
@@ -36,11 +37,14 @@ def tile_nnueevaluator_kernel(tc, x, b, offs, out):
         for pair in range(0, BLOCKS, 2):
             for a in range(A):
                 for k in (pair, pair + 1):
-                    picked = windows[k][:].indirect(offsets[:, a * RUN_COLUMNS : (a + 1) * RUN_COLUMNS])
                     grown = sums.tile([P, Q], F32, name="grown")
-                    nc.vector.tensor_tensor(grown[:], picked, acc[k][:], ADD)
+                    result = sums.tile([P, Q], F32, name="result") if a == A - 1 else None
+                    for q0, q1 in HALVES if (k, a) == (BLOCKS - 1, A - 1) else WHOLE_RUN:
+                        entries = offsets[:, (a * Q + q0) // 16 : (a * Q + q1) // 16]
+                        nc.vector.tensor_tensor(
+                            grown[:, q0:q1], windows[k][:].indirect(entries), acc[k][:, q0:q1], ADD
+                        )
+                        if a == A - 1:
+                            nc.scalar.activation(result[:, q0:q1], grown[:, q0:q1], RELU)
+                            nc.sync.dma_start(out_blocks[k][:, q0:q1], result[:, q0:q1])
                     acc[k] = grown
-            for k in (pair, pair + 1):
-                result = sums.tile([P, Q], F32, name="result")
-                nc.scalar.activation(result[:], acc[k][:], RELU)
-                nc.sync.dma_start(out_blocks[k], result[:])

@@ -1,4 +1,5 @@
 import concourse.mybir as mybir
+from concourse.masks import make_identity
 
 F32 = mybir.dt.float32
 U16 = mybir.dt.uint16
@@ -21,6 +22,8 @@ def tile_nnueevaluator_kernel(tc, x, b, offs, out):
     with (
         tc.tile_pool(name="held", bufs=1) as held,
         tc.tile_pool(name="sums", bufs=6) as sums,
+        tc.tile_pool(name="lanes", bufs=4) as lanes,
+        tc.psum_pool(name="psum", bufs=2) as psum,
     ):
         bias = held.tile([P, BLOCKS], F32, name="bias")
         nc.sync.dma_start(bias[:], b.rearrange("(p k) o -> p (k o)", k=BLOCKS))
@@ -29,22 +32,41 @@ def tile_nnueevaluator_kernel(tc, x, b, offs, out):
         windows = [held.tile([P, S], F32, name=f"window{k}") for k in range(BLOCKS)]
         for k in range(BLOCKS):
             nc.scalar.dma_start(windows[k][:], x_blocks[k])
+        identity = held.tile([P, P], F32, name="identity")
+        make_identity(nc, identity[:])
 
-        acc = [held.tile([P, Q], F32, name=f"start{k}") for k in range(BLOCKS)]
-        for k in range(BLOCKS):
+        pair_sum = [held.tile([P, 2 * Q], F32, name=f"half_bias{k}") for k in (0, 1)]
+        for k in (0, 1):
+            nc.vector.tensor_scalar_mul(pair_sum[k][:], bias[:, k : k + 1].to_broadcast([P, 2 * Q]), 0.5)
+        acc = {}
+        for k in (2, 3):
+            acc[k] = held.tile([P, Q], F32, name=f"start{k}")
             nc.scalar.activation(acc[k][:], bias[:, k : k + 1].to_broadcast([P, Q]), COPY)
 
-        for pair in range(0, BLOCKS, 2):
-            for a in range(A):
-                for k in (pair, pair + 1):
-                    grown = sums.tile([P, Q], F32, name="grown")
-                    result = sums.tile([P, Q], F32, name="result") if a == A - 1 else None
-                    for q0, q1 in HALVES if (k, a) == (BLOCKS - 1, A - 1) else WHOLE_RUN:
-                        entries = offsets[:, (a * Q + q0) // 16 : (a * Q + q1) // 16]
-                        nc.vector.tensor_tensor(
-                            grown[:, q0:q1], windows[k][:].indirect(entries), acc[k][:, q0:q1], ADD
-                        )
-                        if a == A - 1:
-                            nc.scalar.activation(result[:, q0:q1], grown[:, q0:q1], RELU)
-                            nc.sync.dma_start(out_blocks[k][:, q0:q1], result[:, q0:q1])
-                    acc[k] = grown
+        for a in range(0, A, 2):
+            for k in (0, 1):
+                entries = offsets[:, a * Q // 16 : (a + 2) * Q // 16]
+                grown_pair = lanes.tile([P, 2 * Q], F32, name="grown_pair")
+                nc.vector.tensor_tensor(grown_pair[:], windows[k][:].indirect(entries), pair_sum[k][:], ADD)
+                pair_sum[k] = grown_pair
+        for k in (0, 1):
+            merged = psum.tile([P, Q], F32, name="merged")
+            nc.tensor.matmul(merged[:], identity[:], pair_sum[k][:, :Q], start=True, stop=False)
+            nc.tensor.matmul(merged[:], identity[:], pair_sum[k][:, Q:], start=False, stop=True)
+            result = sums.tile([P, Q], F32, name="result")
+            nc.scalar.activation(result[:], merged[:], RELU)
+            nc.sync.dma_start(out_blocks[k], result[:])
+
+        for a in range(A):
+            for k in (2, 3):
+                grown = sums.tile([P, Q], F32, name="grown")
+                result = sums.tile([P, Q], F32, name="result") if a == A - 1 else None
+                for q0, q1 in HALVES if (k, a) == (BLOCKS - 1, A - 1) else WHOLE_RUN:
+                    entries = offsets[:, (a * Q + q0) // 16 : (a * Q + q1) // 16]
+                    nc.vector.tensor_tensor(
+                        grown[:, q0:q1], windows[k][:].indirect(entries), acc[k][:, q0:q1], ADD
+                    )
+                    if a == A - 1:
+                        nc.scalar.activation(result[:, q0:q1], grown[:, q0:q1], RELU)
+                        nc.sync.dma_start(out_blocks[k][:, q0:q1], result[:, q0:q1])
+                acc[k] = grown

@@ -36,8 +36,8 @@ def tile_nnueevaluator_kernel(tc, x, b, offs, out):
         make_identity(nc, identity[:])
 
         pair_sum = [held.tile([P, 2 * Q], F32, name=f"half_bias{k}") for k in (0, 1)]
-        for k in (0, 1):
-            nc.vector.tensor_scalar_mul(pair_sum[k][:], bias[:, k : k + 1].to_broadcast([P, 2 * Q]), 0.5)
+        nc.vector.tensor_scalar_mul(pair_sum[0][:], bias[:, 0:1].to_broadcast([P, 2 * Q]), 0.5)
+        nc.scalar.activation(pair_sum[1][:], bias[:, 1:2].to_broadcast([P, 2 * Q]), COPY, scale=0.5)
         acc = {}
         for k in (2, 3):
             acc[k] = held.tile([P, Q], F32, name=f"start{k}")

@@ -11,6 +11,7 @@ P = 128
 C, S = 512, 1024
 A, Q = 8, 512
 BLOCKS = C // P
+FIRST_LANE_RUNS = 4
 WHOLE_RUN = ((0, Q),)
 HALVES = ((0, Q // 2), (Q // 2, Q))
 
@@ -35,33 +36,46 @@ def tile_nnueevaluator_kernel(tc, x, b, offs, out):
         identity = held.tile([P, P], F32, name="identity")
         make_identity(nc, identity[:])
 
-        pair_sum = [held.tile([P, 2 * Q], F32, name=f"half_bias{k}") for k in (0, 1)]
+        pair_sum = [held.tile([P, 2 * Q], F32, name=f"half_bias{k}") for k in range(BLOCKS)]
         nc.vector.tensor_scalar_mul(pair_sum[0][:], bias[:, 0:1].to_broadcast([P, 2 * Q]), 0.5)
-        nc.scalar.activation(pair_sum[1][:], bias[:, 1:2].to_broadcast([P, 2 * Q]), COPY, scale=0.5)
-        acc = {}
-        for k in (2, 3):
-            acc[k] = held.tile([P, Q], F32, name=f"start{k}")
-            nc.scalar.activation(acc[k][:], bias[:, k : k + 1].to_broadcast([P, Q]), COPY)
+        for k in range(1, BLOCKS):
+            nc.scalar.activation(pair_sum[k][:], bias[:, k : k + 1].to_broadcast([P, 2 * Q]), COPY, scale=0.5)
 
-        for a in range(0, A, 2):
-            for k in (0, 1):
-                entries = offsets[:, a * Q // 16 : (a + 2) * Q // 16]
-                grown_pair = lanes.tile([P, 2 * Q], F32, name="grown_pair")
-                nc.vector.tensor_tensor(grown_pair[:], windows[k][:].indirect(entries), pair_sum[k][:], ADD)
-                pair_sum[k] = grown_pair
-        for k in (0, 1):
+        def add_in_lanes(pair, runs):
+            for a in range(0, runs, 2):
+                for k in pair:
+                    entries = offsets[:, a * Q // 16 : (a + 2) * Q // 16]
+                    grown_pair = lanes.tile([P, 2 * Q], F32, name="grown_pair")
+                    nc.vector.tensor_tensor(
+                        grown_pair[:], windows[k][:].indirect(entries), pair_sum[k][:], ADD
+                    )
+                    pair_sum[k] = grown_pair
+
+        def merge_lanes(k):
             merged = psum.tile([P, Q], F32, name="merged")
             nc.tensor.matmul(merged[:], identity[:], pair_sum[k][:, :Q], start=True, stop=False)
             nc.tensor.matmul(merged[:], identity[:], pair_sum[k][:, Q:], start=False, stop=True)
+            return merged
+
+        add_in_lanes((0, 1), FIRST_LANE_RUNS)
+        acc = {}
+        for k in (0, 1):
+            merged = merge_lanes(k)
+            acc[k] = sums.tile([P, Q], F32, name="merged_sum")
+            nc.scalar.activation(acc[k][:], merged[:], COPY)
+
+        add_in_lanes((2, 3), A)
+        for k in (2, 3):
+            merged = merge_lanes(k)
             result = sums.tile([P, Q], F32, name="result")
             nc.scalar.activation(result[:], merged[:], RELU)
             nc.sync.dma_start(out_blocks[k], result[:])
 
-        for a in range(A):
-            for k in (2, 3):
+        for a in range(FIRST_LANE_RUNS, A):
+            for k in (0, 1):
                 grown = sums.tile([P, Q], F32, name="grown")
                 result = sums.tile([P, Q], F32, name="result") if a == A - 1 else None
-                for q0, q1 in HALVES if (k, a) == (BLOCKS - 1, A - 1) else WHOLE_RUN:
+                for q0, q1 in HALVES if (k, a) == (1, A - 1) else WHOLE_RUN:
                     entries = offsets[:, (a * Q + q0) // 16 : (a * Q + q1) // 16]
                     nc.vector.tensor_tensor(
                         grown[:, q0:q1], windows[k][:].indirect(entries), acc[k][:, q0:q1], ADD

@@ -81,6 +81,9 @@ def tile_nnueevaluator_kernel(tc, x, b, offs, out):
                         grown[:, q0:q1], windows[k][:].indirect(entries), acc[k][:, q0:q1], ADD
                     )
                     if a == A - 1:
-                        nc.scalar.activation(result[:, q0:q1], grown[:, q0:q1], RELU)
+                        if (k, q1) == (1, Q):
+                            nc.vector.tensor_scalar_max(result[:, q0:q1], grown[:, q0:q1], 0.0)
+                        else:
+                            nc.scalar.activation(result[:, q0:q1], grown[:, q0:q1], RELU)
                         nc.sync.dma_start(out_blocks[k][:, q0:q1], result[:, q0:q1])
                 acc[k] = grown

@@ -22,9 +22,9 @@ def tile_nnueevaluator_kernel(tc, x, b, offs, out):
     out_blocks = out.rearrange("(p k) q -> k p q", k=BLOCKS)
     with (
         tc.tile_pool(name="held", bufs=1) as held,
-        tc.tile_pool(name="sums", bufs=6) as sums,
-        tc.tile_pool(name="lanes", bufs=4) as lanes,
-        tc.psum_pool(name="psum", bufs=2) as psum,
+        tc.tile_pool(name="sums", bufs=A) as sums,
+        tc.tile_pool(name="lanes", bufs=(FIRST_LANE_RUNS + A)) as lanes,
+        tc.psum_pool(name="psum", bufs=BLOCKS) as psum,
     ):
         bias = held.tile([P, BLOCKS], F32, name="bias")
         nc.sync.dma_start(bias[:], b.rearrange("(p k) o -> p (k o)", k=BLOCKS))

@@ -72,10 +72,12 @@ def tile_nnueevaluator_kernel(tc, x, b, offs, out):
             nc.sync.dma_start(out_blocks[k], result[:])
 
         for a in range(FIRST_LANE_RUNS, A):
-            for k in (0, 1):
-                grown = sums.tile([P, Q], F32, name="grown")
-                result = sums.tile([P, Q], F32, name="result") if a == A - 1 else None
-                for q0, q1 in HALVES if (k, a) == (1, A - 1) else WHOLE_RUN:
+            grown_of = {k: sums.tile([P, Q], F32, name="grown") for k in (0, 1)}
+            result_of = {k: sums.tile([P, Q], F32, name="result") for k in (0, 1)} if a == A - 1 else None
+            for q0, q1 in HALVES if a == A - 1 else WHOLE_RUN:
+                for k in (0, 1):
+                    grown = grown_of[k]
+                    result = result_of[k] if a == A - 1 else None
                     entries = offsets[:, (a * Q + q0) // 16 : (a * Q + q1) // 16]
                     nc.vector.tensor_tensor(
                         grown[:, q0:q1], windows[k][:].indirect(entries), acc[k][:, q0:q1], ADD
@@ -86,4 +88,4 @@ def tile_nnueevaluator_kernel(tc, x, b, offs, out):
                         else:
                             nc.scalar.activation(result[:, q0:q1], grown[:, q0:q1], RELU)
                         nc.sync.dma_start(out_blocks[k][:, q0:q1], result[:, q0:q1])
-                acc[k] = grown
+            acc = grown_of

@@ -12,8 +12,6 @@ C, S = 512, 1024
 A, Q = 8, 512
 BLOCKS = C // P
 FIRST_LANE_RUNS = 4
-WHOLE_RUN = ((0, Q),)
-HALVES = ((0, Q // 2), (Q // 2, Q))
 
 
 def tile_nnueevaluator_kernel(tc, x, b, offs, out):
@@ -71,21 +69,27 @@ def tile_nnueevaluator_kernel(tc, x, b, offs, out):
             nc.scalar.activation(result[:], merged[:], RELU)
             nc.sync.dma_start(out_blocks[k], result[:])
 
-        for a in range(FIRST_LANE_RUNS, A):
-            grown_of = {k: sums.tile([P, Q], F32, name="grown") for k in (0, 1)}
-            result_of = {k: sums.tile([P, Q], F32, name="result") for k in (0, 1)} if a == A - 1 else None
-            for q0, q1 in HALVES if a == A - 1 else WHOLE_RUN:
-                for k in (0, 1):
-                    grown = grown_of[k]
-                    result = result_of[k] if a == A - 1 else None
-                    entries = offsets[:, (a * Q + q0) // 16 : (a * Q + q1) // 16]
-                    nc.vector.tensor_tensor(
-                        grown[:, q0:q1], windows[k][:].indirect(entries), acc[k][:, q0:q1], ADD
-                    )
-                    if a == A - 1:
-                        if (k, q1) == (1, Q):
-                            nc.vector.tensor_scalar_max(result[:, q0:q1], grown[:, q0:q1], 0.0)
-                        else:
-                            nc.scalar.activation(result[:, q0:q1], grown[:, q0:q1], RELU)
-                        nc.sync.dma_start(out_blocks[k][:, q0:q1], result[:, q0:q1])
-            acc = grown_of
+        def add_piece(k, a, q0, q1, grown):
+            entries = offsets[:, (a * Q + q0) // 16 : (a * Q + q1) // 16]
+            nc.vector.tensor_tensor(
+                grown[:, q0:q1], windows[k][:].indirect(entries), acc[k][:, q0:q1], ADD
+            )
+
+        for a in range(FIRST_LANE_RUNS, A - 1):
+            for k in (0, 1):
+                grown = sums.tile([P, Q], F32, name="grown")
+                add_piece(k, a, 0, Q, grown)
+                acc[k] = grown
+
+        last = {k: sums.tile([P, Q], F32, name="grown") for k in (0, 1)}
+        result = {k: sums.tile([P, Q], F32, name="result") for k in (0, 1)}
+        for k, q0, q1 in ((0, 0, Q // 2), (1, 0, Q // 2), (0, Q // 2, Q)):
+            add_piece(k, A - 1, q0, q1, last[k])
+            nc.scalar.activation(result[k][:, q0:q1], last[k][:, q0:q1], RELU)
+            nc.sync.dma_start(out_blocks[k][:, q0:q1], result[k][:, q0:q1])
+        quarters = ((Q // 2, 3 * Q // 4), (3 * Q // 4, Q))
+        for q0, q1 in quarters:
+            add_piece(1, A - 1, q0, q1, last[1])
+        for q0, q1 in quarters:
+            nc.vector.tensor_scalar_max(result[1][:, q0:q1], last[1][:, q0:q1], 0.0)
+            nc.sync.dma_start(out_blocks[1][:, q0:q1], result[1][:, q0:q1])

@@ -81,12 +81,19 @@ def tile_nnueevaluator_kernel(tc, x, b, offs, out):
                 add_piece(k, a, 0, Q, grown)
                 acc[k] = grown
 
+        halves = ((0, Q // 2), (Q // 2, Q))
         last = {k: sums.tile([P, Q], F32, name="grown") for k in (0, 1)}
         result = {k: sums.tile([P, Q], F32, name="result") for k in (0, 1)}
-        for k, q0, q1 in ((0, 0, Q // 2), (1, 0, Q // 2), (0, Q // 2, Q)):
-            add_piece(k, A - 1, q0, q1, last[k])
+
+        def relu_and_store(k, q0, q1):
             nc.scalar.activation(result[k][:, q0:q1], last[k][:, q0:q1], RELU)
             nc.sync.dma_start(out_blocks[k][:, q0:q1], result[k][:, q0:q1])
+
+        add_piece(0, A - 1, 0, Q, last[0])
+        for q0, q1 in halves:
+            relu_and_store(0, q0, q1)
+        add_piece(1, A - 1, 0, Q // 2, last[1])
+        relu_and_store(1, 0, Q // 2)
         quarters = ((Q // 2, 3 * Q // 4), (3 * Q // 4, Q))
         for q0, q1 in quarters:
             add_piece(1, A - 1, q0, q1, last[1])

@@ -11,7 +11,7 @@ P = 128
 C, S = 512, 1024
 A, Q = 8, 512
 BLOCKS = C // P
-FIRST_LANE_RUNS = 4
+LANE_RUNS = {0: 6, 1: 4}
 
 
 def tile_nnueevaluator_kernel(tc, x, b, offs, out):
@@ -21,7 +21,7 @@ def tile_nnueevaluator_kernel(tc, x, b, offs, out):
     with (
         tc.tile_pool(name="held", bufs=1) as held,
         tc.tile_pool(name="sums", bufs=A) as sums,
-        tc.tile_pool(name="lanes", bufs=(FIRST_LANE_RUNS + A)) as lanes,
+        tc.tile_pool(name="lanes", bufs=(LANE_RUNS[0] // 2 + LANE_RUNS[1] // 2 + A)) as lanes,
         tc.psum_pool(name="psum", bufs=BLOCKS) as psum,
     ):
         bias = held.tile([P, BLOCKS], F32, name="bias")
@@ -39,15 +39,13 @@ def tile_nnueevaluator_kernel(tc, x, b, offs, out):
         for k in range(1, BLOCKS):
             nc.scalar.activation(pair_sum[k][:], bias[:, k : k + 1].to_broadcast([P, 2 * Q]), COPY, scale=0.5)
 
-        def add_in_lanes(pair, runs):
-            for a in range(0, runs, 2):
-                for k in pair:
-                    entries = offsets[:, a * Q // 16 : (a + 2) * Q // 16]
-                    grown_pair = lanes.tile([P, 2 * Q], F32, name="grown_pair")
-                    nc.vector.tensor_tensor(
-                        grown_pair[:], windows[k][:].indirect(entries), pair_sum[k][:], ADD
-                    )
-                    pair_sum[k] = grown_pair
+        def add_pair(k, a):
+            entries = offsets[:, a * Q // 16 : (a + 2) * Q // 16]
+            grown_pair = lanes.tile([P, 2 * Q], F32, name="grown_pair")
+            nc.vector.tensor_tensor(
+                grown_pair[:], windows[k][:].indirect(entries), pair_sum[k][:], ADD
+            )
+            pair_sum[k] = grown_pair
 
         def merge_lanes(k):
             merged = psum.tile([P, Q], F32, name="merged")
@@ -55,19 +53,15 @@ def tile_nnueevaluator_kernel(tc, x, b, offs, out):
             nc.tensor.matmul(merged[:], identity[:], pair_sum[k][:, Q:], start=False, stop=True)
             return merged
 
-        add_in_lanes((0, 1), FIRST_LANE_RUNS)
+        for a in range(0, LANE_RUNS[0], 2):
+            for k in (0, 1):
+                if a < LANE_RUNS[k]:
+                    add_pair(k, a)
         acc = {}
-        for k in (0, 1):
+        for k in (1, 0):
             merged = merge_lanes(k)
             acc[k] = sums.tile([P, Q], F32, name="merged_sum")
             nc.scalar.activation(acc[k][:], merged[:], COPY)
-
-        add_in_lanes((2, 3), A)
-        for k in (2, 3):
-            merged = merge_lanes(k)
-            result = sums.tile([P, Q], F32, name="result")
-            nc.scalar.activation(result[:], merged[:], RELU)
-            nc.sync.dma_start(out_blocks[k], result[:])
 
         def add_piece(k, a, q0, q1, grown):
             entries = offsets[:, (a * Q + q0) // 16 : (a * Q + q1) // 16]
@@ -75,11 +69,26 @@ def tile_nnueevaluator_kernel(tc, x, b, offs, out):
                 grown[:, q0:q1], windows[k][:].indirect(entries), acc[k][:, q0:q1], ADD
             )
 
-        for a in range(FIRST_LANE_RUNS, A - 1):
-            for k in (0, 1):
-                grown = sums.tile([P, Q], F32, name="grown")
-                add_piece(k, a, 0, Q, grown)
-                acc[k] = grown
+        def add_run(k, a):
+            grown = sums.tile([P, Q], F32, name="grown")
+            add_piece(k, a, 0, Q, grown)
+            acc[k] = grown
+
+        for a in range(0, A - 2, 2):
+            for k in (2, 3):
+                add_pair(k, a)
+        add_pair(2, A - 2)
+        add_run(1, LANE_RUNS[1])
+        add_pair(3, A - 2)
+        for k in (2, 3):
+            merged = merge_lanes(k)
+            result = sums.tile([P, Q], F32, name="result")
+            nc.scalar.activation(result[:], merged[:], RELU)
+            nc.sync.dma_start(out_blocks[k], result[:])
+
+        add_run(1, LANE_RUNS[1] + 1)
+        for k in (0, 1):
+            add_run(k, A - 2)
 
         halves = ((0, Q // 2), (Q // 2, Q))
         last = {k: sums.tile([P, Q], F32, name="grown") for k in (0, 1)}

@@ -90,19 +90,14 @@ def tile_nnueevaluator_kernel(tc, x, b, offs, out):
         for k in (0, 1):
             add_run(k, A - 2)
 
-        halves = ((0, Q // 2), (Q // 2, Q))
         last = {k: sums.tile([P, Q], F32, name="grown") for k in (0, 1)}
         result = {k: sums.tile([P, Q], F32, name="result") for k in (0, 1)}
-
-        def relu_and_store(k, q0, q1):
-            nc.scalar.activation(result[k][:, q0:q1], last[k][:, q0:q1], RELU)
-            nc.sync.dma_start(out_blocks[k][:, q0:q1], result[k][:, q0:q1])
-
-        add_piece(0, A - 1, 0, Q, last[0])
-        for q0, q1 in halves:
-            relu_and_store(0, q0, q1)
-        add_piece(1, A - 1, 0, Q // 2, last[1])
-        relu_and_store(1, 0, Q // 2)
+        for k, h0 in ((0, 0), (1, 0), (0, Q // 2)):
+            add_piece(k, A - 1, h0, h0 + Q // 2, last[k])
+            for q0 in (h0, h0 + Q // 4):
+                q1 = q0 + Q // 4
+                nc.scalar.activation(result[k][:, q0:q1], last[k][:, q0:q1], RELU)
+                nc.sync.dma_start(out_blocks[k][:, q0:q1], result[k][:, q0:q1])
         quarters = ((Q // 2, 3 * Q // 4), (3 * Q // 4, Q))
         for q0, q1 in quarters:
             add_piece(1, A - 1, q0, q1, last[1])

import concourse.mybir as mybir
from concourse.masks import make_identity

F32 = mybir.dt.float32
U16 = mybir.dt.uint16
ADD = mybir.AluOpType.add
COPY = mybir.ActivationFunctionType.Copy
RELU = mybir.ActivationFunctionType.Relu

P = 128
C, S = 512, 1024
A, Q = 8, 512
BLOCKS = C // P
LANE_RUNS = {0: 6, 1: 4}


def tile_nnueevaluator_kernel(tc, x, b, offs, out):
    nc = tc.nc
    x_blocks = x.rearrange("(p k) s -> k p s", k=BLOCKS)
    out_blocks = out.rearrange("(p k) q -> k p q", k=BLOCKS)
    with (
        tc.tile_pool(name="held", bufs=1) as held,
        tc.tile_pool(name="sums", bufs=A) as sums,
        tc.tile_pool(name="lanes", bufs=(LANE_RUNS[0] // 2 + LANE_RUNS[1] // 2 + A)) as lanes,
        tc.psum_pool(name="psum", bufs=BLOCKS) as psum,
    ):
        bias = held.tile([P, BLOCKS], F32, name="bias")
        nc.sync.dma_start(bias[:], b.rearrange("(p k) o -> p (k o)", k=BLOCKS))
        offsets = held.tile([P, A * Q // 16], U16, name="offsets")
        nc.sync.dma_start(offsets[:], offs)
        windows = [held.tile([P, S], F32, name=f"window{k}") for k in range(BLOCKS)]
        for k in range(BLOCKS):
            nc.scalar.dma_start(windows[k][:], x_blocks[k])
        identity = held.tile([P, P], F32, name="identity")
        make_identity(nc, identity[:])

        pair_sum = [held.tile([P, 2 * Q], F32, name=f"half_bias{k}") for k in range(BLOCKS)]
        nc.vector.tensor_scalar_mul(pair_sum[0][:], bias[:, 0:1].to_broadcast([P, 2 * Q]), 0.5)
        for k in range(1, BLOCKS):
            nc.scalar.activation(pair_sum[k][:], bias[:, k : k + 1].to_broadcast([P, 2 * Q]), COPY, scale=0.5)

        def add_pair(k, a):
            entries = offsets[:, a * Q // 16 : (a + 2) * Q // 16]
            grown_pair = lanes.tile([P, 2 * Q], F32, name="grown_pair")
            nc.vector.tensor_tensor(
                grown_pair[:], windows[k][:].indirect(entries), pair_sum[k][:], ADD
            )
            pair_sum[k] = grown_pair

        def merge_lanes(k):
            merged = psum.tile([P, Q], F32, name="merged")
            nc.tensor.matmul(merged[:], identity[:], pair_sum[k][:, :Q], start=True, stop=False)
            nc.tensor.matmul(merged[:], identity[:], pair_sum[k][:, Q:], start=False, stop=True)
            return merged

        for a in range(0, LANE_RUNS[0], 2):
            for k in (0, 1):
                if a < LANE_RUNS[k]:
                    add_pair(k, a)
        acc = {}
        for k in (1, 0):
            merged = merge_lanes(k)
            acc[k] = sums.tile([P, Q], F32, name="merged_sum")
            nc.scalar.activation(acc[k][:], merged[:], COPY)

        def add_piece(k, a, q0, q1, grown):
            entries = offsets[:, (a * Q + q0) // 16 : (a * Q + q1) // 16]
            nc.vector.tensor_tensor(
                grown[:, q0:q1], windows[k][:].indirect(entries), acc[k][:, q0:q1], ADD
            )

        def add_run(k, a):
            grown = sums.tile([P, Q], F32, name="grown")
            add_piece(k, a, 0, Q, grown)
            acc[k] = grown

        for a in range(0, A - 2, 2):
            for k in (2, 3):
                add_pair(k, a)
        add_pair(2, A - 2)
        add_run(1, LANE_RUNS[1])
        add_pair(3, A - 2)
        for k in (2, 3):
            merged = merge_lanes(k)
            result = sums.tile([P, Q], F32, name="result")
            nc.scalar.activation(result[:], merged[:], RELU)
            nc.sync.dma_start(out_blocks[k], result[:])

        add_run(1, LANE_RUNS[1] + 1)
        for k in (0, 1):
            add_run(k, A - 2)

        last = {k: sums.tile([P, Q], F32, name="grown") for k in (0, 1)}
        result = {k: sums.tile([P, Q], F32, name="result") for k in (0, 1)}
        for k, h0 in ((0, 0), (1, 0), (0, Q // 2)):
            add_piece(k, A - 1, h0, h0 + Q // 2, last[k])
            for q0 in (h0, h0 + Q // 4):
                q1 = q0 + Q // 4
                nc.scalar.activation(result[k][:, q0:q1], last[k][:, q0:q1], RELU)
                nc.sync.dma_start(out_blocks[k][:, q0:q1], result[k][:, q0:q1])
        quarters = ((Q // 2, 3 * Q // 4), (3 * Q // 4, Q))
        for q0, q1 in quarters:
            add_piece(1, A - 1, q0, q1, last[1])
        for q0, q1 in quarters:
            nc.vector.tensor_scalar_max(result[1][:, q0:q1], last[1][:, q0:q1], 0.0)
            nc.sync.dma_start(out_blocks[1][:, q0:q1], result[1][:, q0:q1])
